import numpy as np
import ml_dtypes


def mxq(x, axis, fmt="e4m3"):
    dtype, down = {"e4m3": (ml_dtypes.float8_e4m3fn, 7), "e5m2": (ml_dtypes.float8_e5m2, 14)}[fmt]
    v = np.moveaxis(np.asarray(x, np.float32).astype(ml_dtypes.bfloat16).astype(np.float64), axis, -1)
    blocks = v.reshape(v.shape[:-1] + (-1, 32))
    amax = np.abs(blocks).max(-1, keepdims=True)
    byte = np.maximum(np.where(amax > 0, np.frexp(amax)[1] - 1 + 127, 0) - down, 1)
    scale = np.exp2(byte - 127.0)
    codes = (blocks / scale).astype(np.float32).astype(dtype).astype(np.float64)
    return np.moveaxis((codes * scale).reshape(v.shape), -1, axis)


WIDE = False


def mx_kscale(k):
    if not WIDE:
        return np.ones(k)
    levels = np.array([10, -10, 5, -5, 0])
    a = np.random.permutation(np.resize(levels, k // 512 * 4)).reshape(k // 512, 4)
    idx = np.arange(k)
    return np.exp2(a[idx // 512, idx % 128 // 32])


BF16 = ml_dtypes.bfloat16


def bf(x):
    return np.asarray(x, np.float32).astype(BF16)


def f64(x):
    return np.asarray(x).astype(np.float64)


B, C, H, W = 1, 1024, 32, 32
INTER = C // 2
HW = H * W
HW2 = HW // 2
SP = np.sqrt(2.0 / np.sqrt(C))


def setup_inputs():
    s = mx_kscale(C)
    t = mx_kscale(INTER)
    return {"q": bf(np.random.standard_normal((B, C, H, W)) * s[None, :, None, None]),
            "k": bf(np.random.standard_normal((B, C, H, W)) * s[None, :, None, None]),
            "W_phi": bf(np.random.standard_normal((INTER, C)) * SP / np.sqrt(C) * t[:, None] / s[None, :]),
            "W_theta": bf(np.random.standard_normal((INTER, C)) * SP / np.sqrt(C) / t[:, None] / s[None, :])}


def reference(q, k, W_phi, W_theta):
    qf = f64(q).reshape(B, C, HW)
    kf = f64(k).reshape(B, C, HW)
    phi = (mxq(f64(W_phi), 1, "e4m3") @ mxq(qf, 1, "e4m3")).reshape(B, C, HW2)
    theta = (mxq(f64(W_theta), 1, "e4m3") @ mxq(kf, 1, "e4m3")).reshape(B, C, HW2)
    return mxq(theta, 1, "e4m3").transpose(0, 2, 1) @ mxq(phi, 1, "e4m3")

@@ -1,0 +1,180 @@
+from contextlib import ExitStack
+
+import concourse.mybir as mybir
+from concourse.masks import make_identity
+
+BF16 = mybir.dt.bfloat16
+F32 = mybir.dt.float32
+U32 = mybir.dt.uint32
+U8 = mybir.dt.uint8
+FP8X4 = mybir.dt.float8_e4m3fn_x4
+
+P = 128
+PACK = 4
+K_PASS = P * PACK
+
+CHANNELS = 1024
+INTER = 512
+PIXELS = 1024
+HALF = PIXELS // 2
+CHANNEL_PASSES = CHANNELS // K_PASS
+FOLD_PASSES = 2 * INTER // K_PASS
+O_PER_FOLD_PASS = INTER // FOLD_PASSES
+WORDS_PER_PASS = K_PASS // 2
+CHUNK = 128
+CHUNKS = HALF // CHUNK
+RUN = 4
+
+FLOPS = 2 * (2 * INTER * CHANNELS * PIXELS) + 2 * HALF * HALF * 2 * INTER
+
+
+def load_map(nc, keep, x, name):
+    rows = x.rearrange("b c h w -> (b c) (h w)")
+    raw = keep.tile([P, CHANNEL_PASSES, PACK, PIXELS], BF16, name=name + "_raw")
+    for g in range(CHANNEL_PASSES):
+        nc.sync.dma_start(
+            out=raw[:, g, :, :],
+            in_=rows[g * K_PASS : (g + 1) * K_PASS, :].rearrange("(p t) w -> p t w", t=PACK),
+        )
+    return raw
+
+
+def load_weights(nc, keep, w, name):
+    rows = keep.tile([P, FOLD_PASSES, 2, CHANNELS], BF16, name=name + "_rows")
+    nc.sync.dma_start(out=rows[:], in_=w.rearrange("(f p e) c -> p f e c", f=FOLD_PASSES, e=2))
+    return rows
+
+
+def mx_tiles(keep, passes, columns, name):
+    values = keep.tile([P, passes, columns, PACK], BF16, name=name + "_values", align_bytes=64)
+    codes = keep.tile([P, passes, columns], U32, name=name + "_codes", align_bytes=64)
+    scales = keep.tile([P, passes, columns], U8, name=name + "_scales", align_bytes=64)
+    return values, codes, scales
+
+
+def quantise(nc, operand, g, columns):
+    values, codes, scales = operand
+    nc.vector.quantize_mx(
+        out=codes[:, g, columns].bitcast(FP8X4),
+        scales=scales[:, g, columns],
+        in_=values[:, g, columns, :].rearrange("p w t -> p (w t)"),
+    )
+
+
+def regroup(nc, operand, raw, g, columns):
+    values = operand[0]
+    nc.vector.tensor_copy(
+        out=values[:, g, columns, :].rearrange("p (c i) t -> p c t i", i=RUN),
+        in_=raw[:, g, :, columns].rearrange("p t (c i) -> p c t i", i=RUN),
+    )
+
+
+def transpose_weights(nc, psum_w, identity, rows, operand):
+    values = operand[0]
+    words = rows[:].bitcast(F32)
+    word_pairs = values[:].bitcast(F32)
+    for g in range(CHANNEL_PASSES):
+        for f in range(FOLD_PASSES):
+            bank = psum_w.tile([P, 2, O_PER_FOLD_PASS], F32, name="w_bank")
+            for u in range(2):
+                for e in range(2):
+                    nc.tensor.transpose(
+                        bank[:, u, e * P : (e + 1) * P],
+                        words[:, f, e, g * WORDS_PER_PASS + u : (g + 1) * WORDS_PER_PASS : 2],
+                        identity[:],
+                    )
+            columns = slice(f * O_PER_FOLD_PASS, (f + 1) * O_PER_FOLD_PASS)
+            nc.scalar.copy(
+                out=word_pairs[:, g, columns, :], in_=bank[:].rearrange("p u o -> p o u")
+            )
+
+
+def project_chunk(nc, psum_p, weights, pixels, folded, f, chunk):
+    w_codes, w_scales = weights[1], weights[2]
+    x_codes, x_scales = pixels[1], pixels[2]
+    bank = psum_p.tile([P, PACK, CHUNK], F32, name="p_bank")
+    for e in range(2):
+        o_cols = slice(f * O_PER_FOLD_PASS + e * P, f * O_PER_FOLD_PASS + (e + 1) * P)
+        for j in range(2):
+            x_cols = slice(j * HALF + chunk * CHUNK, j * HALF + (chunk + 1) * CHUNK)
+            for g in range(CHANNEL_PASSES):
+                nc.tensor.matmul_mx(
+                    out=bank[:, 2 * e + j, :],
+                    lhsT=w_codes[:, g, o_cols].bitcast(FP8X4),
+                    lhsT_scale=w_scales[:, g, o_cols],
+                    rhs=x_codes[:, g, x_cols].bitcast(FP8X4),
+                    rhs_scale=x_scales[:, g, x_cols],
+                    start=(g == 0),
+                    stop=(g == CHANNEL_PASSES - 1),
+                )
+    nc.scalar.copy(
+        out=folded[0][:, f, chunk * CHUNK : (chunk + 1) * CHUNK, :],
+        in_=bank[:].rearrange("p t m -> p m t"),
+    )
+
+
+def tile_nonlocalblock_pa_kernel(tc, q, k, W_phi, W_theta, out):
+    nc = tc.nc
+    with ExitStack() as ctx:
+        keep = ctx.enter_context(tc.tile_pool(name="keep", bufs=1))
+        psum_w = ctx.enter_context(tc.psum_pool(name="psum_w", bufs=2))
+        psum_p = ctx.enter_context(tc.psum_pool(name="psum_p", bufs=4))
+        psum_o = ctx.enter_context(tc.psum_pool(name="psum_o", bufs=2))
+
+        q_raw = load_map(nc, keep, q, "q")
+        w_phi_rows = load_weights(nc, keep, W_phi, "w_phi")
+        w_theta_rows = load_weights(nc, keep, W_theta, "w_theta")
+        k_raw = load_map(nc, keep, k, "k")
+
+        identity = keep.tile([P, P], F32, name="identity")
+        make_identity(nc, identity[:])
+
+        q_mx = mx_tiles(keep, CHANNEL_PASSES, PIXELS, "q")
+        k_mx = mx_tiles(keep, CHANNEL_PASSES, PIXELS, "k")
+        w_phi_mx = mx_tiles(keep, CHANNEL_PASSES, INTER, "w_phi")
+        w_theta_mx = mx_tiles(keep, CHANNEL_PASSES, INTER, "w_theta")
+        phi_mx = mx_tiles(keep, FOLD_PASSES, HALF, "phi")
+        theta_mx = mx_tiles(keep, FOLD_PASSES, HALF, "theta")
+
+        for raw, x_mx, rows, w_mx, folded in (
+            (q_raw, q_mx, w_phi_rows, w_phi_mx, phi_mx),
+            (k_raw, k_mx, w_theta_rows, w_theta_mx, theta_mx),
+        ):
+            for j in range(2):
+                regroup(nc, x_mx, raw, 0, slice(j * HALF, (j + 1) * HALF))
+            for j in range(2):
+                quantise(nc, x_mx, 0, slice(j * HALF, (j + 1) * HALF))
+
+            transpose_weights(nc, psum_w, identity, rows, w_mx)
+            for g in range(CHANNEL_PASSES):
+                quantise(nc, w_mx, g, slice(0, INTER))
+
+            for chunk in range(CHUNKS):
+                halves = [
+                    slice(j * HALF + chunk * CHUNK, j * HALF + (chunk + 1) * CHUNK)
+                    for j in range(2)
+                ]
+                for columns in halves:
+                    regroup(nc, x_mx, raw, 1, columns)
+                for columns in halves:
+                    quantise(nc, x_mx, 1, columns)
+                m_cols = slice(chunk * CHUNK, (chunk + 1) * CHUNK)
+                for f in range(FOLD_PASSES):
+                    project_chunk(nc, psum_p, w_mx, x_mx, folded, f, chunk)
+                    quantise(nc, folded, f, m_cols)
+
+                if folded is theta_mx:
+                    acc = psum_o.tile([P, HALF], F32, name="acc")
+                    for f in range(FOLD_PASSES):
+                        nc.tensor.matmul_mx(
+                            out=acc[:],
+                            lhsT=theta_mx[1][:, f, m_cols].bitcast(FP8X4),
+                            lhsT_scale=theta_mx[2][:, f, m_cols],
+                            rhs=phi_mx[1][:, f, :].bitcast(FP8X4),
+                            rhs_scale=phi_mx[2][:, f, :],
+                            start=(f == 0),
+                            stop=(f == FOLD_PASSES - 1),
+                        )
+                    result = keep.tile([P, HALF], F32, name="result%d" % chunk)
+                    nc.scalar.copy(out=result[:], in_=acc[:])
+                    nc.sync.dma_start(out=out[0, m_cols, :], in_=result[:])

@@ -23,6 +23,8 @@ O_PER_FOLD_PASS = INTER // FOLD_PASSES
 WORDS_PER_PASS = K_PASS // 2
 CHUNK = 128
 CHUNKS = HALF // CHUNK
+PSUM_BANKS = 8
+BANK = 512
 RUN = 4
 
 FLOPS = 2 * (2 * INTER * CHANNELS * PIXELS) + 2 * HALF * HALF * 2 * INTER
@@ -61,21 +63,29 @@ def quantise(nc, operand, g, columns):
     )
 
 
-def regroup(nc, operand, raw, g, columns):
+def regroup(copy, operand, raw, g, columns):
     values = operand[0]
-    nc.vector.tensor_copy(
+    copy(
         out=values[:, g, columns, :].rearrange("p (c i) t -> p c t i", i=RUN),
         in_=raw[:, g, :, columns].rearrange("p t (c i) -> p c t i", i=RUN),
     )
 
 
-def transpose_weights(nc, psum_w, identity, rows, operand):
+def half(j):
+    return slice(j * HALF, (j + 1) * HALF)
+
+
+def chunk_of_half(j, chunk):
+    return slice(j * HALF + chunk * CHUNK, j * HALF + (chunk + 1) * CHUNK)
+
+
+def transpose_weights(nc, psum, identity, rows, operand):
     values = operand[0]
     words = rows[:].bitcast(F32)
     word_pairs = values[:].bitcast(F32)
     for g in range(CHANNEL_PASSES):
         for f in range(FOLD_PASSES):
-            bank = psum_w.tile([P, 2, O_PER_FOLD_PASS], F32, name="w_bank")
+            bank = psum.tile([P, 2, O_PER_FOLD_PASS], F32, name="bank")
             for u in range(2):
                 for e in range(2):
                     nc.tensor.transpose(
@@ -89,14 +99,14 @@ def transpose_weights(nc, psum_w, identity, rows, operand):
             )
 
 
-def project_chunk(nc, psum_p, weights, pixels, folded, f, chunk):
+def project_chunk(nc, psum, weights, pixels, folded, f, chunk):
     w_codes, w_scales = weights[1], weights[2]
     x_codes, x_scales = pixels[1], pixels[2]
-    bank = psum_p.tile([P, PACK, CHUNK], F32, name="p_bank")
+    bank = psum.tile([P, PACK, CHUNK], F32, name="bank")
     for e in range(2):
         o_cols = slice(f * O_PER_FOLD_PASS + e * P, f * O_PER_FOLD_PASS + (e + 1) * P)
         for j in range(2):
-            x_cols = slice(j * HALF + chunk * CHUNK, j * HALF + (chunk + 1) * CHUNK)
+            x_cols = chunk_of_half(j, chunk)
             for g in range(CHANNEL_PASSES):
                 nc.tensor.matmul_mx(
                     out=bank[:, 2 * e + j, :],
@@ -117,9 +127,8 @@ def tile_nonlocalblock_pa_kernel(tc, q, k, W_phi, W_theta, out):
     nc = tc.nc
     with ExitStack() as ctx:
         keep = ctx.enter_context(tc.tile_pool(name="keep", bufs=1))
-        psum_w = ctx.enter_context(tc.psum_pool(name="psum_w", bufs=2))
-        psum_p = ctx.enter_context(tc.psum_pool(name="psum_p", bufs=4))
-        psum_o = ctx.enter_context(tc.psum_pool(name="psum_o", bufs=2))
+        psum = ctx.enter_context(tc.psum_pool(name="psum", bufs=PSUM_BANKS))
+        ctx.enter_context(tc.manual_schedule())
 
         q_raw = load_map(nc, keep, q, "q")
         w_phi_rows = load_weights(nc, keep, W_phi, "w_phi")
@@ -136,45 +145,59 @@ def tile_nonlocalblock_pa_kernel(tc, q, k, W_phi, W_theta, out):
         phi_mx = mx_tiles(keep, FOLD_PASSES, HALF, "phi")
         theta_mx = mx_tiles(keep, FOLD_PASSES, HALF, "theta")
 
-        for raw, x_mx, rows, w_mx, folded in (
-            (q_raw, q_mx, w_phi_rows, w_phi_mx, phi_mx),
-            (k_raw, k_mx, w_theta_rows, w_theta_mx, theta_mx),
-        ):
+        for g in range(CHANNEL_PASSES):
+            regroup(nc.vector.tensor_copy, q_mx, q_raw, g, half(0))
+            regroup(nc.scalar.copy, q_mx, q_raw, g, half(1))
+        for g in range(CHANNEL_PASSES):
             for j in range(2):
-                regroup(nc, x_mx, raw, 0, slice(j * HALF, (j + 1) * HALF))
-            for j in range(2):
-                quantise(nc, x_mx, 0, slice(j * HALF, (j + 1) * HALF))
+                quantise(nc, q_mx, g, half(j))
 
-            transpose_weights(nc, psum_w, identity, rows, w_mx)
-            for g in range(CHANNEL_PASSES):
-                quantise(nc, w_mx, g, slice(0, INTER))
+        transpose_weights(nc, psum, identity, w_phi_rows, w_phi_mx)
+        for g in range(CHANNEL_PASSES):
+            quantise(nc, w_phi_mx, g, slice(0, INTER))
+        transpose_weights(nc, psum, identity, w_theta_rows, w_theta_mx)
 
-            for chunk in range(CHUNKS):
-                halves = [
-                    slice(j * HALF + chunk * CHUNK, j * HALF + (chunk + 1) * CHUNK)
-                    for j in range(2)
-                ]
-                for columns in halves:
-                    regroup(nc, x_mx, raw, 1, columns)
-                for columns in halves:
-                    quantise(nc, x_mx, 1, columns)
-                m_cols = slice(chunk * CHUNK, (chunk + 1) * CHUNK)
+        for chunk in range(CHUNKS):
+            for f in range(FOLD_PASSES):
+                project_chunk(nc, psum, w_phi_mx, q_mx, phi_mx, f, chunk)
+
+        for j in range(2):
+            regroup(nc.vector.tensor_copy, k_mx, k_raw, 0, half(j))
+        for g in range(CHANNEL_PASSES):
+            quantise(nc, w_theta_mx, g, slice(0, INTER))
+
+        for chunk in range(CHUNKS + 1):
+            if chunk < CHUNKS:
+                for j in range(2):
+                    regroup(nc.vector.tensor_copy, k_mx, k_raw, 1, chunk_of_half(j, chunk))
+            if chunk > 0:
+                for g in range(CHANNEL_PASSES):
+                    for j in range(2):
+                        quantise(nc, k_mx, g, chunk_of_half(j, chunk - 1))
                 for f in range(FOLD_PASSES):
-                    project_chunk(nc, psum_p, w_mx, x_mx, folded, f, chunk)
-                    quantise(nc, folded, f, m_cols)
+                    project_chunk(nc, psum, w_theta_mx, k_mx, theta_mx, f, chunk - 1)
 
-                if folded is theta_mx:
-                    acc = psum_o.tile([P, HALF], F32, name="acc")
-                    for f in range(FOLD_PASSES):
-                        nc.tensor.matmul_mx(
-                            out=acc[:],
-                            lhsT=theta_mx[1][:, f, m_cols].bitcast(FP8X4),
-                            lhsT_scale=theta_mx[2][:, f, m_cols],
-                            rhs=phi_mx[1][:, f, :].bitcast(FP8X4),
-                            rhs_scale=phi_mx[2][:, f, :],
-                            start=(f == 0),
-                            stop=(f == FOLD_PASSES - 1),
-                        )
-                    result = keep.tile([P, HALF], F32, name="result%d" % chunk)
-                    nc.scalar.copy(out=result[:], in_=acc[:])
-                    nc.sync.dma_start(out=out[0, m_cols, :], in_=result[:])
+        for folded in (phi_mx, theta_mx):
+            for chunk in range(CHUNKS):
+                for f in range(FOLD_PASSES):
+                    quantise(nc, folded, f, slice(chunk * CHUNK, (chunk + 1) * CHUNK))
+
+        for chunk in range(CHUNKS):
+            n_rows = slice(chunk * CHUNK, (chunk + 1) * CHUNK)
+            acc = psum.tile([P, BANK], F32, name="bank")
+            for f in range(FOLD_PASSES):
+                nc.tensor.matmul_mx(
+                    out=acc[:],
+                    lhsT=theta_mx[1][:, f, n_rows].bitcast(FP8X4),
+                    lhsT_scale=theta_mx[2][:, f, n_rows],
+                    rhs=phi_mx[1][:, f, :].bitcast(FP8X4),
+                    rhs_scale=phi_mx[2][:, f, :],
+                    start=(f == 0),
+                    stop=(f == FOLD_PASSES - 1),
+                )
+            result = keep.tile([P, HALF], F32, name="result%d" % chunk)
+            if chunk % 2 == 0:
+                nc.scalar.copy(out=result[:], in_=acc[:])
+            else:
+                nc.vector.tensor_copy(out=result[:], in_=acc[:])
+            nc.sync.dma_start(out=out[0, n_rows, :], in_=result[:])

@@ -24,7 +24,7 @@ WORDS_PER_PASS = K_PASS // 2
 CHUNK = 128
 CHUNKS = HALF // CHUNK
 PSUM_BANKS = 8
-BANK = 512
+SIDE = HALF // 2
 RUN = 4
 
 FLOPS = 2 * (2 * INTER * CHANNELS * PIXELS) + 2 * HALF * HALF * 2 * INTER
@@ -43,7 +43,9 @@ def load_map(nc, keep, x, name):
 
 def load_weights(nc, keep, w, name):
     rows = keep.tile([P, FOLD_PASSES, 2, CHANNELS], BF16, name=name + "_rows")
-    nc.sync.dma_start(out=rows[:], in_=w.rearrange("(f p e) c -> p f e c", f=FOLD_PASSES, e=2))
+    by_fold_pass = w.rearrange("(f p e) c -> f p e c", f=FOLD_PASSES, e=2)
+    for f in range(FOLD_PASSES):
+        nc.sync.dma_start(out=rows[:, f, :, :], in_=by_fold_pass[f])
     return rows
 
 
@@ -79,12 +81,16 @@ def chunk_of_half(j, chunk):
     return slice(j * HALF + chunk * CHUNK, j * HALF + (chunk + 1) * CHUNK)
 
 
+def fold_pass(f):
+    return slice(f * O_PER_FOLD_PASS, (f + 1) * O_PER_FOLD_PASS)
+
+
 def transpose_weights(nc, psum, identity, rows, operand):
     values = operand[0]
     words = rows[:].bitcast(F32)
     word_pairs = values[:].bitcast(F32)
-    for g in range(CHANNEL_PASSES):
-        for f in range(FOLD_PASSES):
+    for f in range(FOLD_PASSES):
+        for g in range(CHANNEL_PASSES):
             bank = psum.tile([P, 2, O_PER_FOLD_PASS], F32, name="bank")
             for u in range(2):
                 for e in range(2):
@@ -93,9 +99,8 @@ def transpose_weights(nc, psum, identity, rows, operand):
                         words[:, f, e, g * WORDS_PER_PASS + u : (g + 1) * WORDS_PER_PASS : 2],
                         identity[:],
                     )
-            columns = slice(f * O_PER_FOLD_PASS, (f + 1) * O_PER_FOLD_PASS)
             nc.scalar.copy(
-                out=word_pairs[:, g, columns, :], in_=bank[:].rearrange("p u o -> p o u")
+                out=word_pairs[:, g, fold_pass(f), :], in_=bank[:].rearrange("p u o -> p o u")
             )
 
 
@@ -153,51 +158,50 @@ def tile_nonlocalblock_pa_kernel(tc, q, k, W_phi, W_theta, out):
                 quantise(nc, q_mx, g, half(j))
 
         transpose_weights(nc, psum, identity, w_phi_rows, w_phi_mx)
-        for g in range(CHANNEL_PASSES):
-            quantise(nc, w_phi_mx, g, slice(0, INTER))
+        for f in range(FOLD_PASSES):
+            for g in range(CHANNEL_PASSES):
+                quantise(nc, w_phi_mx, g, fold_pass(f))
         transpose_weights(nc, psum, identity, w_theta_rows, w_theta_mx)
 
         for chunk in range(CHUNKS):
             for f in range(FOLD_PASSES):
                 project_chunk(nc, psum, w_phi_mx, q_mx, phi_mx, f, chunk)
 
-        for j in range(2):
-            regroup(nc.vector.tensor_copy, k_mx, k_raw, 0, half(j))
-        for g in range(CHANNEL_PASSES):
-            quantise(nc, w_theta_mx, g, slice(0, INTER))
+        for i in range(2):
+            for g in range(CHANNEL_PASSES):
+                quantise(nc, w_theta_mx, g, fold_pass(i))
+            regroup(nc.vector.tensor_copy, k_mx, k_raw, 0, half(i))
 
-        for chunk in range(CHUNKS + 1):
-            if chunk < CHUNKS:
+        for chunk in range(CHUNKS):
+            for j in range(2):
+                regroup(nc.vector.tensor_copy, k_mx, k_raw, 1, chunk_of_half(j, chunk))
+            for g in range(CHANNEL_PASSES):
                 for j in range(2):
-                    regroup(nc.vector.tensor_copy, k_mx, k_raw, 1, chunk_of_half(j, chunk))
-            if chunk > 0:
-                for g in range(CHANNEL_PASSES):
-                    for j in range(2):
-                        quantise(nc, k_mx, g, chunk_of_half(j, chunk - 1))
-                for f in range(FOLD_PASSES):
-                    project_chunk(nc, psum, w_theta_mx, k_mx, theta_mx, f, chunk - 1)
+                    quantise(nc, k_mx, g, chunk_of_half(j, chunk))
+            for f in range(FOLD_PASSES):
+                project_chunk(nc, psum, w_theta_mx, k_mx, theta_mx, f, chunk)
 
-        for folded in (phi_mx, theta_mx):
-            for chunk in range(CHUNKS):
-                for f in range(FOLD_PASSES):
-                    quantise(nc, folded, f, slice(chunk * CHUNK, (chunk + 1) * CHUNK))
+        for f in range(FOLD_PASSES):
+            quantise(nc, phi_mx, f, slice(0, HALF))
+        for chunk in range(CHUNKS):
+            for f in range(FOLD_PASSES):
+                quantise(nc, theta_mx, f, slice(chunk * CHUNK, (chunk + 1) * CHUNK))
 
         for chunk in range(CHUNKS):
             n_rows = slice(chunk * CHUNK, (chunk + 1) * CHUNK)
-            acc = psum.tile([P, BANK], F32, name="bank")
-            for f in range(FOLD_PASSES):
-                nc.tensor.matmul_mx(
-                    out=acc[:],
-                    lhsT=theta_mx[1][:, f, n_rows].bitcast(FP8X4),
-                    lhsT_scale=theta_mx[2][:, f, n_rows],
-                    rhs=phi_mx[1][:, f, :].bitcast(FP8X4),
-                    rhs_scale=phi_mx[2][:, f, :],
-                    start=(f == 0),
-                    stop=(f == FOLD_PASSES - 1),
-                )
             result = keep.tile([P, HALF], F32, name="result%d" % chunk)
-            if chunk % 2 == 0:
-                nc.scalar.copy(out=result[:], in_=acc[:])
-            else:
-                nc.vector.tensor_copy(out=result[:], in_=acc[:])
+            for side, copy in enumerate((nc.scalar.copy, nc.vector.tensor_copy)):
+                m_cols = slice(side * SIDE, (side + 1) * SIDE)
+                acc = psum.tile([P, SIDE], F32, name="bank")
+                for f in range(FOLD_PASSES):
+                    nc.tensor.matmul_mx(
+                        out=acc[:],
+                        lhsT=theta_mx[1][:, f, n_rows].bitcast(FP8X4),
+                        lhsT_scale=theta_mx[2][:, f, n_rows],
+                        rhs=phi_mx[1][:, f, m_cols].bitcast(FP8X4),
+                        rhs_scale=phi_mx[2][:, f, m_cols],
+                        start=(f == 0),
+                        stop=(f == FOLD_PASSES - 1),
+                    )
+                copy(out=result[:, m_cols], in_=acc[:])
             nc.sync.dma_start(out=out[0, n_rows, :], in_=result[:])

@@ -204,4 +204,4 @@ def tile_nonlocalblock_pa_kernel(tc, q, k, W_phi, W_theta, out):
                         stop=(f == FOLD_PASSES - 1),
                     )
                 copy(out=result[:, m_cols], in_=acc[:])
-            nc.sync.dma_start(out=out[0, n_rows, :], in_=result[:])
+                nc.sync.dma_start(out=out[0, n_rows, m_cols], in_=result[:, m_cols])

@@ -25,7 +25,7 @@ CHUNK = 128
 CHUNKS = HALF // CHUNK
 PSUM_BANKS = 8
 SIDE = HALF // 2
-RUN = 4
+RUN = 8
 
 FLOPS = 2 * (2 * INTER * CHANNELS * PIXELS) + 2 * HALF * HALF * 2 * INTER
 

@@ -16,7 +16,8 @@ K_PASS = P * PACK
 CHANNELS = 1024
 INTER = 512
 PIXELS = 1024
-HALF = PIXELS // 2
+HALVES = 2
+HALF = PIXELS // HALVES
 CHANNEL_PASSES = CHANNELS // K_PASS
 FOLD_PASSES = 2 * INTER // K_PASS
 O_PER_FOLD_PASS = INTER // FOLD_PASSES
@@ -32,10 +33,10 @@ FLOPS = 2 * (2 * INTER * CHANNELS * PIXELS) + 2 * HALF * HALF * 2 * INTER
 
 def load_map(nc, keep, x, name):
     rows = x.rearrange("b c h w -> (b c) (h w)")
-    raw = keep.tile([P, CHANNEL_PASSES, PACK, PIXELS], BF16, name=name + "_raw")
+    raw = keep.tile([P, CHANNEL_PASSES, PACK, HALVES, CHUNKS, CHUNK], BF16, name=name + "_raw")
     for g in range(CHANNEL_PASSES):
         nc.sync.dma_start(
-            out=raw[:, g, :, :],
+            out=raw[:, g, :, :, :, :].rearrange("p t j n i -> p t (j n i)"),
             in_=rows[g * K_PASS : (g + 1) * K_PASS, :].rearrange("(p t) w -> p t w", t=PACK),
         )
     return raw
@@ -50,9 +51,9 @@ def load_weights(nc, keep, w, name):
 
 
 def mx_tiles(keep, passes, columns, name):
-    values = keep.tile([P, passes, columns, PACK], BF16, name=name + "_values", align_bytes=64)
-    codes = keep.tile([P, passes, columns], U32, name=name + "_codes", align_bytes=64)
-    scales = keep.tile([P, passes, columns], U8, name=name + "_scales", align_bytes=64)
+    values = keep.tile([P, passes] + columns + [PACK], BF16, name=name + "_values", align_bytes=64)
+    codes = keep.tile([P, passes] + columns, U32, name=name + "_codes", align_bytes=64)
+    scales = keep.tile([P, passes] + columns, U8, name=name + "_scales", align_bytes=64)
     return values, codes, scales
 
 
@@ -65,20 +66,34 @@ def quantise(nc, operand, g, columns):
     )
 
 
-def regroup(copy, operand, raw, g, columns):
-    values = operand[0]
-    copy(
-        out=values[:, g, columns, :].rearrange("p (c i) t -> p c t i", i=RUN),
-        in_=raw[:, g, :, columns].rearrange("p t (c i) -> p c t i", i=RUN),
+def quantise_chunks(nc, operand, g, chunks):
+    values, codes, scales = operand
+    nc.vector.quantize_mx(
+        out=codes[:, g, chunks, :, :].rearrange("p n j i -> p (n j i)").bitcast(FP8X4),
+        scales=scales[:, g, chunks, :, :].rearrange("p n j i -> p (n j i)"),
+        in_=values[:, g, chunks, :, :, :].rearrange("p n j i t -> p (n j i t)"),
     )
 
 
-def half(j):
-    return slice(j * HALF, (j + 1) * HALF)
+def quantise_half_chunk(nc, operand, g, chunk, j):
+    values, codes, scales = operand
+    nc.vector.quantize_mx(
+        out=codes[:, g, chunk, j, :].bitcast(FP8X4),
+        scales=scales[:, g, chunk, j, :],
+        in_=values[:, g, chunk, j, :, :].rearrange("p i t -> p (i t)"),
+    )
 
 
-def chunk_of_half(j, chunk):
-    return slice(j * HALF + chunk * CHUNK, j * HALF + (chunk + 1) * CHUNK)
+def regroup(copy, operand, raw, g, j, chunks):
+    values = operand[0]
+    copy(
+        out=values[:, g, chunks, j, :, :].rearrange("p n (c i) t -> p n c t i", i=RUN),
+        in_=raw[:, g, :, j, chunks, :].rearrange("p t n (c i) -> p n c t i", i=RUN),
+    )
+
+
+def one(index):
+    return slice(index, index + 1)
 
 
 def fold_pass(f):
@@ -110,18 +125,16 @@ def project_chunk(nc, psum, weights, pixels, folded, f, chunk):
     bank = psum.tile([P, PACK, CHUNK], F32, name="bank")
     for e in range(2):
         o_cols = slice(f * O_PER_FOLD_PASS + e * P, f * O_PER_FOLD_PASS + (e + 1) * P)
-        for j in range(2):
-            x_cols = chunk_of_half(j, chunk)
-            for g in range(CHANNEL_PASSES):
-                nc.tensor.matmul_mx(
-                    out=bank[:, 2 * e + j, :],
-                    lhsT=w_codes[:, g, o_cols].bitcast(FP8X4),
-                    lhsT_scale=w_scales[:, g, o_cols],
-                    rhs=x_codes[:, g, x_cols].bitcast(FP8X4),
-                    rhs_scale=x_scales[:, g, x_cols],
-                    start=(g == 0),
-                    stop=(g == CHANNEL_PASSES - 1),
-                )
+        for g in range(CHANNEL_PASSES):
+            nc.tensor.matmul_mx(
+                out=bank[:, 2 * e : 2 * e + 2, :].rearrange("p j m -> p (j m)"),
+                lhsT=w_codes[:, g, o_cols].bitcast(FP8X4),
+                lhsT_scale=w_scales[:, g, o_cols],
+                rhs=x_codes[:, g, chunk, :, :].rearrange("p j m -> p (j m)").bitcast(FP8X4),
+                rhs_scale=x_scales[:, g, chunk, :, :].rearrange("p j m -> p (j m)"),
+                start=(g == 0),
+                stop=(g == CHANNEL_PASSES - 1),
+            )
     nc.scalar.copy(
         out=folded[0][:, f, chunk * CHUNK : (chunk + 1) * CHUNK, :],
         in_=bank[:].rearrange("p t m -> p m t"),
@@ -143,19 +156,20 @@ def tile_nonlocalblock_pa_kernel(tc, q, k, W_phi, W_theta, out):
         identity = keep.tile([P, P], F32, name="identity")
         make_identity(nc, identity[:])
 
-        q_mx = mx_tiles(keep, CHANNEL_PASSES, PIXELS, "q")
-        k_mx = mx_tiles(keep, CHANNEL_PASSES, PIXELS, "k")
-        w_phi_mx = mx_tiles(keep, CHANNEL_PASSES, INTER, "w_phi")
-        w_theta_mx = mx_tiles(keep, CHANNEL_PASSES, INTER, "w_theta")
-        phi_mx = mx_tiles(keep, FOLD_PASSES, HALF, "phi")
-        theta_mx = mx_tiles(keep, FOLD_PASSES, HALF, "theta")
+        q_mx = mx_tiles(keep, CHANNEL_PASSES, [CHUNKS, HALVES, CHUNK], "q")
+        k_mx = mx_tiles(keep, CHANNEL_PASSES, [CHUNKS, HALVES, CHUNK], "k")
+        w_phi_mx = mx_tiles(keep, CHANNEL_PASSES, [INTER], "w_phi")
+        w_theta_mx = mx_tiles(keep, CHANNEL_PASSES, [INTER], "w_theta")
+        phi_mx = mx_tiles(keep, FOLD_PASSES, [HALF], "phi")
+        theta_mx = mx_tiles(keep, FOLD_PASSES, [HALF], "theta")
+        all_chunks = slice(0, CHUNKS)
 
         for g in range(CHANNEL_PASSES):
-            regroup(nc.vector.tensor_copy, q_mx, q_raw, g, half(0))
-            regroup(nc.scalar.copy, q_mx, q_raw, g, half(1))
+            regroup(nc.vector.tensor_copy, q_mx, q_raw, g, 0, all_chunks)
+            regroup(nc.scalar.copy, q_mx, q_raw, g, 1, all_chunks)
         for g in range(CHANNEL_PASSES):
-            for j in range(2):
-                quantise(nc, q_mx, g, half(j))
+            for first in range(0, CHUNKS, 2):
+                quantise_chunks(nc, q_mx, g, slice(first, first + 2))
 
         transpose_weights(nc, psum, identity, w_phi_rows, w_phi_mx)
         for f in range(FOLD_PASSES):
@@ -170,14 +184,14 @@ def tile_nonlocalblock_pa_kernel(tc, q, k, W_phi, W_theta, out):
         for i in range(2):
             for g in range(CHANNEL_PASSES):
                 quantise(nc, w_theta_mx, g, fold_pass(i))
-            regroup(nc.vector.tensor_copy, k_mx, k_raw, 0, half(i))
+            regroup(nc.vector.tensor_copy, k_mx, k_raw, 0, i, all_chunks)
 
         for chunk in range(CHUNKS):
-            for j in range(2):
-                regroup(nc.vector.tensor_copy, k_mx, k_raw, 1, chunk_of_half(j, chunk))
+            for j in range(HALVES):
+                regroup(nc.vector.tensor_copy, k_mx, k_raw, 1, j, one(chunk))
             for g in range(CHANNEL_PASSES):
-                for j in range(2):
-                    quantise(nc, k_mx, g, chunk_of_half(j, chunk))
+                for j in range(HALVES):
+                    quantise_half_chunk(nc, k_mx, g, chunk, j)
             for f in range(FOLD_PASSES):
                 project_chunk(nc, psum, w_theta_mx, k_mx, theta_mx, f, chunk)
 

@@ -119,7 +119,7 @@ def transpose_weights(nc, psum, identity, rows, operand):
             )
 
 
-def project_chunk(nc, psum, weights, pixels, folded, f, chunk):
+def project_sums(nc, psum, weights, pixels, f, chunk):
     w_codes, w_scales = weights[1], weights[2]
     x_codes, x_scales = pixels[1], pixels[2]
     bank = psum.tile([P, PACK, CHUNK], F32, name="bank")
@@ -135,10 +135,42 @@ def project_chunk(nc, psum, weights, pixels, folded, f, chunk):
                 start=(g == 0),
                 stop=(g == CHANNEL_PASSES - 1),
             )
+    return bank
+
+
+def round_sums(nc, bank, folded, f, chunk):
     nc.scalar.copy(
         out=folded[0][:, f, chunk * CHUNK : (chunk + 1) * CHUNK, :],
         in_=bank[:].rearrange("p t m -> p m t"),
     )
+
+
+def project_chunk(nc, psum, weights, pixels, folded, f, chunk):
+    round_sums(nc, project_sums(nc, psum, weights, pixels, f, chunk), folded, f, chunk)
+
+
+def out_sums(nc, psum, theta_mx, phi_mx, chunk, side):
+    n_rows = slice(chunk * CHUNK, (chunk + 1) * CHUNK)
+    m_cols = slice(side * SIDE, (side + 1) * SIDE)
+    acc = psum.tile([P, SIDE], F32, name="bank")
+    for f in range(FOLD_PASSES):
+        nc.tensor.matmul_mx(
+            out=acc[:],
+            lhsT=theta_mx[1][:, f, n_rows].bitcast(FP8X4),
+            lhsT_scale=theta_mx[2][:, f, n_rows],
+            rhs=phi_mx[1][:, f, m_cols].bitcast(FP8X4),
+            rhs_scale=phi_mx[2][:, f, m_cols],
+            start=(f == 0),
+            stop=(f == FOLD_PASSES - 1),
+        )
+    return acc
+
+
+def store_sums(nc, copy, acc, result, out, chunk, side):
+    n_rows = slice(chunk * CHUNK, (chunk + 1) * CHUNK)
+    m_cols = slice(side * SIDE, (side + 1) * SIDE)
+    copy(out=result[:, m_cols], in_=acc[:])
+    nc.sync.dma_start(out=out[0, n_rows, m_cols], in_=result[:, m_cols])
 
 
 def tile_nonlocalblock_pa_kernel(tc, q, k, W_phi, W_theta, out):
@@ -192,30 +224,32 @@ def tile_nonlocalblock_pa_kernel(tc, q, k, W_phi, W_theta, out):
             for g in range(CHANNEL_PASSES):
                 for j in range(HALVES):
                     quantise_half_chunk(nc, k_mx, g, chunk, j)
-            for f in range(FOLD_PASSES):
-                project_chunk(nc, psum, w_theta_mx, k_mx, theta_mx, f, chunk)
+            if chunk < CHUNKS - 1:
+                for f in range(FOLD_PASSES):
+                    project_chunk(nc, psum, w_theta_mx, k_mx, theta_mx, f, chunk)
+        project_chunk(nc, psum, w_theta_mx, k_mx, theta_mx, 0, CHUNKS - 1)
+        last_theta = project_sums(nc, psum, w_theta_mx, k_mx, 1, CHUNKS - 1)
 
-        for f in range(FOLD_PASSES):
-            quantise(nc, phi_mx, f, slice(0, HALF))
-        for chunk in range(CHUNKS):
+        results = [keep.tile([P, HALF], F32, name="result%d" % chunk) for chunk in range(CHUNKS)]
+
+        def quantise_phi(side):
+            for f in range(FOLD_PASSES):
+                quantise(nc, phi_mx, f, slice(side * SIDE, (side + 1) * SIDE))
+
+        def quantise_theta(chunk):
             for f in range(FOLD_PASSES):
                 quantise(nc, theta_mx, f, slice(chunk * CHUNK, (chunk + 1) * CHUNK))
 
-        for chunk in range(CHUNKS):
-            n_rows = slice(chunk * CHUNK, (chunk + 1) * CHUNK)
-            result = keep.tile([P, HALF], F32, name="result%d" % chunk)
+        quantise_phi(0)
+        quantise_theta(0)
+        store_sums(nc, nc.scalar.copy, out_sums(nc, psum, theta_mx, phi_mx, 0, 0), results[0], out, 0, 0)
+        round_sums(nc, last_theta, theta_mx, 1, CHUNKS - 1)
+        quantise_phi(1)
+        right_of_first = out_sums(nc, psum, theta_mx, phi_mx, 0, 1)
+        for chunk in range(1, CHUNKS - 1):
+            quantise_theta(chunk)
+        store_sums(nc, nc.vector.tensor_copy, right_of_first, results[0], out, 0, 1)
+        quantise_theta(CHUNKS - 1)
+        for chunk in range(1, CHUNKS):
             for side, copy in enumerate((nc.scalar.copy, nc.vector.tensor_copy)):
-                m_cols = slice(side * SIDE, (side + 1) * SIDE)
-                acc = psum.tile([P, SIDE], F32, name="bank")
-                for f in range(FOLD_PASSES):
-                    nc.tensor.matmul_mx(
-                        out=acc[:],
-                        lhsT=theta_mx[1][:, f, n_rows].bitcast(FP8X4),
-                        lhsT_scale=theta_mx[2][:, f, n_rows],
-                        rhs=phi_mx[1][:, f, m_cols].bitcast(FP8X4),
-                        rhs_scale=phi_mx[2][:, f, m_cols],
-                        start=(f == 0),
-                        stop=(f == FOLD_PASSES - 1),
-                    )
-                copy(out=result[:, m_cols], in_=acc[:])
-                nc.sync.dma_start(out=out[0, n_rows, m_cols], in_=result[:, m_cols])
+                store_sums(nc, copy, out_sums(nc, psum, theta_mx, phi_mx, chunk, side), results[chunk], out, chunk, side)

from contextlib import ExitStack

import concourse.mybir as mybir
from concourse.masks import make_identity

BF16 = mybir.dt.bfloat16
F32 = mybir.dt.float32
U32 = mybir.dt.uint32
U8 = mybir.dt.uint8
FP8X4 = mybir.dt.float8_e4m3fn_x4

P = 128
PACK = 4
K_PASS = P * PACK

CHANNELS = 1024
INTER = 512
PIXELS = 1024
HALVES = 2
HALF = PIXELS // HALVES
CHANNEL_PASSES = CHANNELS // K_PASS
FOLD_PASSES = 2 * INTER // K_PASS
O_PER_FOLD_PASS = INTER // FOLD_PASSES
WORDS_PER_PASS = K_PASS // 2
CHUNK = 128
CHUNKS = HALF // CHUNK
PSUM_BANKS = 8
SIDE = HALF // 2
RUN = 8

FLOPS = 2 * (2 * INTER * CHANNELS * PIXELS) + 2 * HALF * HALF * 2 * INTER


def load_map(nc, keep, x, name):
    rows = x.rearrange("b c h w -> (b c) (h w)")
    raw = keep.tile([P, CHANNEL_PASSES, PACK, HALVES, CHUNKS, CHUNK], BF16, name=name + "_raw")
    for g in range(CHANNEL_PASSES):
        nc.sync.dma_start(
            out=raw[:, g, :, :, :, :].rearrange("p t j n i -> p t (j n i)"),
            in_=rows[g * K_PASS : (g + 1) * K_PASS, :].rearrange("(p t) w -> p t w", t=PACK),
        )
    return raw


def load_weights(nc, keep, w, name):
    rows = keep.tile([P, FOLD_PASSES, 2, CHANNELS], BF16, name=name + "_rows")
    by_fold_pass = w.rearrange("(f p e) c -> f p e c", f=FOLD_PASSES, e=2)
    for f in range(FOLD_PASSES):
        nc.sync.dma_start(out=rows[:, f, :, :], in_=by_fold_pass[f])
    return rows


def mx_tiles(keep, passes, columns, name):
    values = keep.tile([P, passes] + columns + [PACK], BF16, name=name + "_values", align_bytes=64)
    codes = keep.tile([P, passes] + columns, U32, name=name + "_codes", align_bytes=64)
    scales = keep.tile([P, passes] + columns, U8, name=name + "_scales", align_bytes=64)
    return values, codes, scales


def quantise(nc, operand, g, columns):
    values, codes, scales = operand
    nc.vector.quantize_mx(
        out=codes[:, g, columns].bitcast(FP8X4),
        scales=scales[:, g, columns],
        in_=values[:, g, columns, :].rearrange("p w t -> p (w t)"),
    )


def quantise_chunks(nc, operand, g, chunks):
    values, codes, scales = operand
    nc.vector.quantize_mx(
        out=codes[:, g, chunks, :, :].rearrange("p n j i -> p (n j i)").bitcast(FP8X4),
        scales=scales[:, g, chunks, :, :].rearrange("p n j i -> p (n j i)"),
        in_=values[:, g, chunks, :, :, :].rearrange("p n j i t -> p (n j i t)"),
    )


def quantise_half_chunk(nc, operand, g, chunk, j):
    values, codes, scales = operand
    nc.vector.quantize_mx(
        out=codes[:, g, chunk, j, :].bitcast(FP8X4),
        scales=scales[:, g, chunk, j, :],
        in_=values[:, g, chunk, j, :, :].rearrange("p i t -> p (i t)"),
    )


def regroup(copy, operand, raw, g, j, chunks):
    values = operand[0]
    copy(
        out=values[:, g, chunks, j, :, :].rearrange("p n (c i) t -> p n c t i", i=RUN),
        in_=raw[:, g, :, j, chunks, :].rearrange("p t n (c i) -> p n c t i", i=RUN),
    )


def one(index):
    return slice(index, index + 1)


def fold_pass(f):
    return slice(f * O_PER_FOLD_PASS, (f + 1) * O_PER_FOLD_PASS)


def transpose_weights(nc, psum, identity, rows, operand):
    values = operand[0]
    words = rows[:].bitcast(F32)
    word_pairs = values[:].bitcast(F32)
    for f in range(FOLD_PASSES):
        for g in range(CHANNEL_PASSES):
            bank = psum.tile([P, 2, O_PER_FOLD_PASS], F32, name="bank")
            for u in range(2):
                for e in range(2):
                    nc.tensor.transpose(
                        bank[:, u, e * P : (e + 1) * P],
                        words[:, f, e, g * WORDS_PER_PASS + u : (g + 1) * WORDS_PER_PASS : 2],
                        identity[:],
                    )
            nc.scalar.copy(
                out=word_pairs[:, g, fold_pass(f), :], in_=bank[:].rearrange("p u o -> p o u")
            )


def project_sums(nc, psum, weights, pixels, f, chunk):
    w_codes, w_scales = weights[1], weights[2]
    x_codes, x_scales = pixels[1], pixels[2]
    bank = psum.tile([P, PACK, CHUNK], F32, name="bank")
    for e in range(2):
        o_cols = slice(f * O_PER_FOLD_PASS + e * P, f * O_PER_FOLD_PASS + (e + 1) * P)
        for g in range(CHANNEL_PASSES):
            nc.tensor.matmul_mx(
                out=bank[:, 2 * e : 2 * e + 2, :].rearrange("p j m -> p (j m)"),
                lhsT=w_codes[:, g, o_cols].bitcast(FP8X4),
                lhsT_scale=w_scales[:, g, o_cols],
                rhs=x_codes[:, g, chunk, :, :].rearrange("p j m -> p (j m)").bitcast(FP8X4),
                rhs_scale=x_scales[:, g, chunk, :, :].rearrange("p j m -> p (j m)"),
                start=(g == 0),
                stop=(g == CHANNEL_PASSES - 1),
            )
    return bank


def round_sums(nc, bank, folded, f, chunk):
    nc.scalar.copy(
        out=folded[0][:, f, chunk * CHUNK : (chunk + 1) * CHUNK, :],
        in_=bank[:].rearrange("p t m -> p m t"),
    )


def project_chunk(nc, psum, weights, pixels, folded, f, chunk):
    round_sums(nc, project_sums(nc, psum, weights, pixels, f, chunk), folded, f, chunk)


def out_sums(nc, psum, theta_mx, phi_mx, chunk, side):
    n_rows = slice(chunk * CHUNK, (chunk + 1) * CHUNK)
    m_cols = slice(side * SIDE, (side + 1) * SIDE)
    acc = psum.tile([P, SIDE], F32, name="bank")
    for f in range(FOLD_PASSES):
        nc.tensor.matmul_mx(
            out=acc[:],
            lhsT=theta_mx[1][:, f, n_rows].bitcast(FP8X4),
            lhsT_scale=theta_mx[2][:, f, n_rows],
            rhs=phi_mx[1][:, f, m_cols].bitcast(FP8X4),
            rhs_scale=phi_mx[2][:, f, m_cols],
            start=(f == 0),
            stop=(f == FOLD_PASSES - 1),
        )
    return acc


def store_sums(nc, copy, acc, result, out, chunk, side):
    n_rows = slice(chunk * CHUNK, (chunk + 1) * CHUNK)
    m_cols = slice(side * SIDE, (side + 1) * SIDE)
    copy(out=result[:, m_cols], in_=acc[:])
    nc.sync.dma_start(out=out[0, n_rows, m_cols], in_=result[:, m_cols])


def tile_nonlocalblock_pa_kernel(tc, q, k, W_phi, W_theta, out):
    nc = tc.nc
    with ExitStack() as ctx:
        keep = ctx.enter_context(tc.tile_pool(name="keep", bufs=1))
        psum = ctx.enter_context(tc.psum_pool(name="psum", bufs=PSUM_BANKS))
        ctx.enter_context(tc.manual_schedule())

        q_raw = load_map(nc, keep, q, "q")
        w_phi_rows = load_weights(nc, keep, W_phi, "w_phi")
        w_theta_rows = load_weights(nc, keep, W_theta, "w_theta")
        k_raw = load_map(nc, keep, k, "k")

        identity = keep.tile([P, P], F32, name="identity")
        make_identity(nc, identity[:])

        q_mx = mx_tiles(keep, CHANNEL_PASSES, [CHUNKS, HALVES, CHUNK], "q")
        k_mx = mx_tiles(keep, CHANNEL_PASSES, [CHUNKS, HALVES, CHUNK], "k")
        w_phi_mx = mx_tiles(keep, CHANNEL_PASSES, [INTER], "w_phi")
        w_theta_mx = mx_tiles(keep, CHANNEL_PASSES, [INTER], "w_theta")
        phi_mx = mx_tiles(keep, FOLD_PASSES, [HALF], "phi")
        theta_mx = mx_tiles(keep, FOLD_PASSES, [HALF], "theta")
        all_chunks = slice(0, CHUNKS)

        for g in range(CHANNEL_PASSES):
            regroup(nc.vector.tensor_copy, q_mx, q_raw, g, 0, all_chunks)
            regroup(nc.scalar.copy, q_mx, q_raw, g, 1, all_chunks)
        for g in range(CHANNEL_PASSES):
            for first in range(0, CHUNKS, 2):
                quantise_chunks(nc, q_mx, g, slice(first, first + 2))

        transpose_weights(nc, psum, identity, w_phi_rows, w_phi_mx)
        for f in range(FOLD_PASSES):
            for g in range(CHANNEL_PASSES):
                quantise(nc, w_phi_mx, g, fold_pass(f))
        transpose_weights(nc, psum, identity, w_theta_rows, w_theta_mx)

        for chunk in range(CHUNKS):
            for f in range(FOLD_PASSES):
                project_chunk(nc, psum, w_phi_mx, q_mx, phi_mx, f, chunk)

        for i in range(2):
            for g in range(CHANNEL_PASSES):
                quantise(nc, w_theta_mx, g, fold_pass(i))
            regroup(nc.vector.tensor_copy, k_mx, k_raw, 0, i, all_chunks)

        for chunk in range(CHUNKS):
            for j in range(HALVES):
                regroup(nc.vector.tensor_copy, k_mx, k_raw, 1, j, one(chunk))
            for g in range(CHANNEL_PASSES):
                for j in range(HALVES):
                    quantise_half_chunk(nc, k_mx, g, chunk, j)
            if chunk < CHUNKS - 1:
                for f in range(FOLD_PASSES):
                    project_chunk(nc, psum, w_theta_mx, k_mx, theta_mx, f, chunk)
        project_chunk(nc, psum, w_theta_mx, k_mx, theta_mx, 0, CHUNKS - 1)
        last_theta = project_sums(nc, psum, w_theta_mx, k_mx, 1, CHUNKS - 1)

        results = [keep.tile([P, HALF], F32, name="result%d" % chunk) for chunk in range(CHUNKS)]

        def quantise_phi(side):
            for f in range(FOLD_PASSES):
                quantise(nc, phi_mx, f, slice(side * SIDE, (side + 1) * SIDE))

        def quantise_theta(chunk):
            for f in range(FOLD_PASSES):
                quantise(nc, theta_mx, f, slice(chunk * CHUNK, (chunk + 1) * CHUNK))

        quantise_phi(0)
        quantise_theta(0)
        store_sums(nc, nc.scalar.copy, out_sums(nc, psum, theta_mx, phi_mx, 0, 0), results[0], out, 0, 0)
        round_sums(nc, last_theta, theta_mx, 1, CHUNKS - 1)
        quantise_phi(1)
        right_of_first = out_sums(nc, psum, theta_mx, phi_mx, 0, 1)
        for chunk in range(1, CHUNKS - 1):
            quantise_theta(chunk)
        store_sums(nc, nc.vector.tensor_copy, right_of_first, results[0], out, 0, 1)
        quantise_theta(CHUNKS - 1)
        for chunk in range(1, CHUNKS):
            for side, copy in enumerate((nc.scalar.copy, nc.vector.tensor_copy)):
                store_sums(nc, copy, out_sums(nc, psum, theta_mx, phi_mx, chunk, side), results[chunk], out, chunk, side)
